import numpy as np
import ml_dtypes


def mxq(x, axis, fmt="e4m3"):
    dtype, down = {"e4m3": (ml_dtypes.float8_e4m3fn, 7), "e5m2": (ml_dtypes.float8_e5m2, 14)}[fmt]
    v = np.moveaxis(np.asarray(x, np.float32).astype(ml_dtypes.bfloat16).astype(np.float64), axis, -1)
    blocks = v.reshape(v.shape[:-1] + (-1, 32))
    amax = np.abs(blocks).max(-1, keepdims=True)
    byte = np.maximum(np.where(amax > 0, np.frexp(amax)[1] - 1 + 127, 0) - down, 1)
    scale = np.exp2(byte - 127.0)
    codes = (blocks / scale).astype(np.float32).astype(dtype).astype(np.float64)
    return np.moveaxis((codes * scale).reshape(v.shape), -1, axis)


WIDE = False


def mx_kscale(k):
    if not WIDE:
        return np.ones(k)
    levels = np.array([10, -10, 5, -5, 0])
    if k % 512:
        return np.exp2(np.random.permutation(np.resize(levels, k // 32))).repeat(32)
    a = np.empty((k // 512, 16))
    for p in range(k // 512):
        a[p, :8] = np.random.permutation(np.resize(levels, 8))
        for g in range(8):
            far = levels[np.abs(levels - a[p, g]) >= 10]
            a[p, g + 8] = far[np.random.randint(len(far))]
    return np.exp2(a.ravel()).repeat(32)


BF16 = ml_dtypes.bfloat16


def bf(x):
    return np.asarray(x, np.float32).astype(BF16)


def f64(x):
    return np.asarray(x).astype(np.float64)


B, L, LV, H = 128, 32, 64, 512
NUM_ITERATIONS = 3
X = 0.25
V = 0.12 * L
A = 0.6 / (np.sqrt(H) * V)


def setup_inputs():
    s = mx_kscale(H)
    return {"text_feat": bf(np.random.standard_normal((B, L, H)) * X * s),
            "vision_proj": bf(np.random.standard_normal((B, 1, H)) * V),
            "Wt": bf(np.random.standard_normal((H, H)) * A / (X * np.sqrt(H)) / s[None, :]),
            "bt": bf(np.random.standard_normal(H) * 0.5 * A)}


def reference(text_feat, vision_proj, Wt, bt):
    vp = f64(vision_proj)
    text_proj = (mxq(f64(text_feat), 2, "e4m3") @ mxq(f64(Wt), 1, "e4m3").T) + f64(bt)
    agreement = np.sum(text_proj * vp, axis=-1, keepdims=True)
    coupling = np.zeros_like(agreement)
    for _ in range(NUM_ITERATIONS - 1):
        coupling = coupling + agreement
    e = np.exp(coupling - coupling.max(axis=1, keepdims=True))
    routing_weights = e / e.sum(axis=1, keepdims=True)
    weighted_vision = routing_weights * vp
    return text_proj, weighted_vision

@@ -1,0 +1,200 @@
+from contextlib import ExitStack
+
+import concourse.mybir as mybir
+from concourse.masks import make_identity
+
+F32 = mybir.dt.float32
+BF16 = mybir.dt.bfloat16
+U32 = mybir.dt.uint32
+U8 = mybir.dt.uint8
+FP8X4 = mybir.dt.float8_e4m3fn_x4
+ALU = mybir.AluOpType
+ACT = mybir.ActivationFunctionType
+
+P = 128
+L = 32
+H = 512
+WORDS = H // 2
+PAIR = 2
+GROUP = 4
+N_GROUPS = L // GROUP
+GPSIMD_SHARE = 2
+
+FLOPS = 2 * P * L * H * H
+
+
+def tile_dynamicroutingfusion_pa_t_kernel(tc, text_feat, vision_proj, Wt, bt, out_0, out_1):
+    nc = tc.nc
+    with ExitStack() as ctx:
+        keep = ctx.enter_context(tc.tile_pool(name="keep", bufs=1))
+        stage = ctx.enter_context(tc.tile_pool(name="stage", bufs=3))
+        psum_t = ctx.enter_context(tc.psum_pool(name="psum_t", bufs=2))
+        psum_acc = ctx.enter_context(tc.psum_pool(name="psum_acc", bufs=6))
+        ctx.enter_context(tc.manual_schedule())
+
+        ident = keep.tile([P, P], F32)
+        ones = keep.tile([P, P], BF16)
+        bt_rows = keep.tile([P, H], BF16)
+        bias = keep.tile([P, H], F32)
+        w_rows = keep.tile([P, GROUP * H], BF16)
+        w_codes = keep.tile([P, H], U32, align_bytes=64)
+        w_scales = keep.tile([P, H], U8, align_bytes=64)
+        text_rows = keep.tile([P, L * H], BF16)
+        x_codes = keep.tile([P, L * P], U32, align_bytes=64)
+        x_scales = keep.tile([P, L * P], U8, align_bytes=64)
+        vp_bf = keep.tile([P, H], BF16)
+        vp = keep.tile([P, H], F32)
+        text_proj = keep.tile([P, L, H], F32)
+        weighted = keep.tile([P, L, H], F32)
+        coupling = keep.tile([P, L], F32)
+        neg_max = keep.tile([P, 1], F32)
+        exps = keep.tile([P, L], F32)
+        exp_sum = keep.tile([P, 1], F32)
+        inv_sum = keep.tile([P, 1], F32)
+        routing = keep.tile([P, L], F32)
+        warm = keep.tile([P, 1], F32)
+
+        def load_pair(rows, source, pair):
+            nc.sync.dma_start(
+                out=rows[:, pair * PAIR * H : (pair + 1) * PAIR * H].rearrange(
+                    "p (c k) -> p c k", c=PAIR
+                ),
+                in_=source[:, pair * PAIR : (pair + 1) * PAIR, :],
+            )
+
+        w_source = Wt.rearrange("(c p) k -> p c k", p=P)
+        nc.vector.memset(bt_rows[:], 0.0)
+        load_pair(w_rows, w_source, 0)
+        nc.sync.dma_start(out=bt_rows[0:1, :], in_=bt.rearrange("(o h) -> o h", o=1))
+        load_pair(w_rows, w_source, 1)
+        load_pair(text_rows, text_feat, 0)
+        load_pair(text_rows, text_feat, 1)
+        nc.sync.dma_start(out=vp_bf[:], in_=vision_proj.rearrange("b o h -> b (o h)"))
+        for pair in range(2, L // PAIR):
+            load_pair(text_rows, text_feat, pair)
+
+        make_identity(nc, ident[:])
+        nc.vector.memset(ones[:], 1.0)
+        nc.vector.memset(warm[:], 0.0)
+        nc.scalar.activation(out=warm[:], in_=warm[:], func=ACT.Exp)
+
+        def regroup(rows, first_tile, copy_out):
+            words = rows[:].bitcast(F32)
+            grouped = stage.tile([P, GROUP * H], BF16, align_bytes=64)
+            grouped_words = grouped[:].bitcast(F32)
+            for pair in range(GROUP // PAIR):
+                bank = psum_t.tile([P, PAIR * WORDS], F32)
+                for j in range(PAIR):
+                    for u in range(2):
+                        col = (first_tile + PAIR * pair + j) * WORDS
+                        nc.tensor.transpose(
+                            bank[:, (2 * j + u) * P : (2 * j + u + 1) * P],
+                            words[:, col + u : col + WORDS : 2],
+                            ident[:],
+                        )
+                copy_out(
+                    out=grouped_words[:, pair * PAIR * WORDS : (pair + 1) * PAIR * WORDS].rearrange(
+                        "p (j r u) -> p j r u", j=PAIR, u=2
+                    ),
+                    in_=bank[:].rearrange("p (j u r) -> p j r u", j=PAIR, u=2),
+                )
+            return grouped
+
+        def quantise(grouped, codes, scales):
+            nc.vector.quantize_mx(out=codes.bitcast(FP8X4), scales=scales, in_=grouped[:])
+
+        def quantise_text(g, grouped):
+            cols = slice(g * GROUP * P, (g + 1) * GROUP * P)
+            quantise(grouped, x_codes[:, cols], x_scales[:, cols])
+
+        def multiply_and_sum(l):
+            acc = psum_acc.tile([P, H], F32)
+            nc.tensor.matmul_mx(
+                out=acc[:],
+                lhsT=x_codes[:, l * P : (l + 1) * P].bitcast(FP8X4),
+                lhsT_scale=x_scales[:, l * P : (l + 1) * P],
+                rhs=w_codes[:].bitcast(FP8X4),
+                rhs_scale=w_scales[:],
+                start=True,
+                stop=True,
+            )
+            nc.vector.scalar_tensor_tensor(
+                out=weighted[:, l, :],
+                in0=acc[:],
+                scalar=2.0,
+                in1=vp[:],
+                op0=ALU.mult,
+                op1=ALU.mult,
+                accum_out=coupling[:, l : l + 1],
+            )
+            return acc
+
+        def add_bias_off_vector(l, acc):
+            nc.scalar.copy(out=text_proj[:, l, :], in_=acc[:])
+            nc.gpsimd.tensor_tensor(
+                out=text_proj[:, l, :], in0=text_proj[:, l, :], in1=bias[:], op=ALU.add
+            )
+
+        def add_bias_on_vector(l, acc):
+            nc.vector.tensor_tensor(out=text_proj[:, l, :], in0=acc[:], in1=bias[:], op=ALU.add)
+
+        def store_text_proj(g):
+            tiles = slice(g * GROUP, (g + 1) * GROUP)
+            nc.sync.dma_start(out=out_0[:, tiles, :], in_=text_proj[:, tiles, :])
+
+        quantise(regroup(w_rows, 0, nc.vector.tensor_copy), w_codes[:], w_scales[:])
+        grouped_of = {0: regroup(text_rows, 0, nc.scalar.copy)}
+        quantise_text(0, grouped_of[0])
+        spread = psum_acc.tile([P, H], F32, tag="acc")
+        nc.tensor.matmul(out=spread[:], lhsT=ones[:], rhs=bt_rows[:], start=True, stop=True)
+        nc.scalar.copy(out=bias[:], in_=spread[:])
+        nc.scalar.copy(out=vp[:], in_=vp_bf[:])
+        grouped_of[1] = regroup(text_rows, GROUP, nc.scalar.copy)
+        waiting = []
+        for g in range(N_GROUPS):
+            for j in range(GROUP):
+                l = g * GROUP + j
+                acc = multiply_and_sum(l)
+                if j == 0 and g + 1 < N_GROUPS:
+                    quantise_text(g + 1, grouped_of[g + 1])
+                if j < GPSIMD_SHARE:
+                    add_bias_off_vector(l, acc)
+                elif g < N_GROUPS - 1:
+                    add_bias_on_vector(l, acc)
+                else:
+                    waiting.append((l, acc))
+            if g < N_GROUPS - 1:
+                store_text_proj(g)
+            if g + 2 < N_GROUPS:
+                grouped_of[g + 2] = regroup(text_rows, (g + 2) * GROUP, nc.scalar.copy)
+
+        nc.vector.tensor_reduce(
+            out=neg_max[:], in_=coupling[:], axis=mybir.AxisListType.X, op=ALU.max, negate=True
+        )
+        nc.scalar.activation(
+            out=exps[:], in_=coupling[:], func=ACT.Exp, bias=neg_max[:], scale=1.0, accum_out=exp_sum[:]
+        )
+        for l, acc in waiting:
+            add_bias_on_vector(l, acc)
+        store_text_proj(N_GROUPS - 1)
+        nc.vector.reciprocal(out=inv_sum[:], in_=exp_sum[:])
+        nc.vector.tensor_scalar(
+            out=routing[:], in0=exps[:], scalar1=inv_sum[:, 0:1], scalar2=None, op0=ALU.mult
+        )
+
+        for g in range(N_GROUPS):
+            for l in range(g * GROUP, (g + 1) * GROUP):
+                if l % 2 == 0:
+                    nc.scalar.activation(
+                        out=weighted[:, l, :], in_=vp[:], func=ACT.Copy, scale=routing[:, l : l + 1]
+                    )
+                else:
+                    nc.vector.tensor_scalar(
+                        out=weighted[:, l, :],
+                        in0=vp[:],
+                        scalar1=routing[:, l : l + 1],
+                        scalar2=None,
+                        op0=ALU.mult,
+                    )
+            tiles = slice(g * GROUP, (g + 1) * GROUP)
+            nc.sync.dma_start(out=out_1[:, tiles, :], in_=weighted[:, tiles, :])

@@ -10,191 +10,389 @@ U8 = mybir.dt.uint8
 FP8X4 = mybir.dt.float8_e4m3fn_x4
 ALU = mybir.AluOpType
 ACT = mybir.ActivationFunctionType
+AXIS_X = mybir.AxisListType.X
 
 P = 128
 L = 32
 H = 512
 WORDS = H // 2
 PAIR = 2
-GROUP = 4
-N_GROUPS = L // GROUP
-GPSIMD_SHARE = 2
+CHUNK = 4
+N_CHUNKS = L // CHUNK
+GROUPS = (16, 32, 32, 32, 16)
+GPSIMD_BIAS = 2
 
 FLOPS = 2 * P * L * H * H
 
 
+def group_table():
+    table = []
+    first_batch = 0
+    first_tile = 0
+    for n in GROUPS:
+        spread = P // n
+        tiles = L // spread
+        table.append((first_batch, n, spread, first_tile, tiles))
+        first_batch += n
+        first_tile += tiles
+    return table
+
+
 def tile_dynamicroutingfusion_pa_t_kernel(tc, text_feat, vision_proj, Wt, bt, out_0, out_1):
     nc = tc.nc
+    groups = group_table()
+    n_groups = len(groups)
+    group_of_tile = {}
+    for q, (b0, n, s, i0, T) in enumerate(groups):
+        for t in range(T):
+            group_of_tile[i0 + t] = q
+    spreads = sorted(set(g[2] for g in groups))
+
     with ExitStack() as ctx:
         keep = ctx.enter_context(tc.tile_pool(name="keep", bufs=1))
         stage = ctx.enter_context(tc.tile_pool(name="stage", bufs=3))
+        small = ctx.enter_context(tc.tile_pool(name="small", bufs=2))
         psum_t = ctx.enter_context(tc.psum_pool(name="psum_t", bufs=2))
-        psum_acc = ctx.enter_context(tc.psum_pool(name="psum_acc", bufs=6))
+        psum_acc = ctx.enter_context(tc.psum_pool(name="psum_acc", bufs=5))
+        psum_misc = ctx.enter_context(tc.psum_pool(name="psum_misc", bufs=1))
         ctx.enter_context(tc.manual_schedule())
 
         ident = keep.tile([P, P], F32)
         ones = keep.tile([P, P], BF16)
         bt_rows = keep.tile([P, H], BF16)
-        bias = keep.tile([P, H], F32)
-        w_rows = keep.tile([P, GROUP * H], BF16)
+        w_rows = keep.tile([P, CHUNK * H], BF16)
         w_codes = keep.tile([P, H], U32, align_bytes=64)
         w_scales = keep.tile([P, H], U8, align_bytes=64)
         text_rows = keep.tile([P, L * H], BF16)
         x_codes = keep.tile([P, L * P], U32, align_bytes=64)
         x_scales = keep.tile([P, L * P], U8, align_bytes=64)
         vp_bf = keep.tile([P, H], BF16)
-        vp = keep.tile([P, H], F32)
+        select = keep.tile([P, n_groups * P], BF16)
+        rows = keep.tile([P, (1 + n_groups) * H], BF16)
         text_proj = keep.tile([P, L, H], F32)
         weighted = keep.tile([P, L, H], F32)
         coupling = keep.tile([P, L], F32)
-        neg_max = keep.tile([P, 1], F32)
         exps = keep.tile([P, L], F32)
-        exp_sum = keep.tile([P, 1], F32)
-        inv_sum = keep.tile([P, 1], F32)
         routing = keep.tile([P, L], F32)
+        neg_max = keep.tile([P, n_groups], F32)
+        exp_sum = keep.tile([P, n_groups], F32)
+        inv_sum = keep.tile([P, n_groups], F32)
         warm = keep.tile([P, 1], F32)
+        block = {}
+        slot_mask = {}
+        for s in spreads:
+            block[s] = keep.tile([P, P], F32, name="block%d" % s)
+            slot_mask[s] = keep.tile([P, s], F32, name="slot_mask%d" % s)
 
-        def load_pair(rows, source, pair):
+        text_flat = text_feat.rearrange("b l k -> (b l) k")
+        out_flat = [o.rearrange("b l h -> (b l) h") for o in (out_0, out_1)]
+
+        def hbm_tiles(flat, first, count):
+            b0, n, s, i0, T = groups[group_of_tile[first]]
+            view = flat[b0 * L : (b0 + n) * L, :].rearrange("(p t) k -> p t k", t=T)
+            return view[:, first - i0 : first - i0 + count, :]
+
+        def load_text(first, count):
             nc.sync.dma_start(
-                out=rows[:, pair * PAIR * H : (pair + 1) * PAIR * H].rearrange(
-                    "p (c k) -> p c k", c=PAIR
-                ),
-                in_=source[:, pair * PAIR : (pair + 1) * PAIR, :],
+                out=text_rows[:, first * H : (first + count) * H].rearrange("p (c k) -> p c k", c=count),
+                in_=hbm_tiles(text_flat, first, count),
             )
 
         w_source = Wt.rearrange("(c p) k -> p c k", p=P)
+
+        def load_w(first, count):
+            nc.sync.dma_start(
+                out=w_rows[:, first * H : (first + count) * H].rearrange("p (c k) -> p c k", c=count),
+                in_=w_source[:, first : first + count, :],
+            )
+
         nc.vector.memset(bt_rows[:], 0.0)
-        load_pair(w_rows, w_source, 0)
+        load_w(0, PAIR)
+        load_w(PAIR, PAIR)
+        load_text(0, PAIR)
         nc.sync.dma_start(out=bt_rows[0:1, :], in_=bt.rearrange("(o h) -> o h", o=1))
-        load_pair(w_rows, w_source, 1)
-        load_pair(text_rows, text_feat, 0)
-        load_pair(text_rows, text_feat, 1)
         nc.sync.dma_start(out=vp_bf[:], in_=vision_proj.rearrange("b o h -> b (o h)"))
-        for pair in range(2, L // PAIR):
-            load_pair(text_rows, text_feat, pair)
+        load_text(PAIR, PAIR)
+        for c in range(1, N_CHUNKS):
+            load_text(c * CHUNK, CHUNK)
 
         make_identity(nc, ident[:])
+        for s in spreads:
+            nc.gpsimd.memset(block[s][:], 0.0)
+            nc.gpsimd.affine_select(
+                out=block[s][:], in_=block[s][:], compare_op=ALU.is_gt, fill=1.0, base=1 - s,
+                pattern=[[-s, P // s], [0, s]], channel_multiplier=1,
+            )
+            nc.gpsimd.affine_select(
+                out=block[s][:], in_=block[s][:], compare_op=ALU.is_ge, fill=0.0, base=0,
+                pattern=[[-s, P // s], [0, s]], channel_multiplier=1,
+            )
         nc.vector.memset(ones[:], 1.0)
         nc.vector.memset(warm[:], 0.0)
         nc.scalar.activation(out=warm[:], in_=warm[:], func=ACT.Exp)
 
-        def regroup(rows, first_tile, copy_out):
-            words = rows[:].bitcast(F32)
-            grouped = stage.tile([P, GROUP * H], BF16, align_bytes=64)
-            grouped_words = grouped[:].bitcast(F32)
-            for pair in range(GROUP // PAIR):
-                bank = psum_t.tile([P, PAIR * WORDS], F32)
-                for j in range(PAIR):
-                    for u in range(2):
-                        col = (first_tile + PAIR * pair + j) * WORDS
-                        nc.tensor.transpose(
-                            bank[:, (2 * j + u) * P : (2 * j + u + 1) * P],
-                            words[:, col + u : col + WORDS : 2],
-                            ident[:],
-                        )
-                copy_out(
-                    out=grouped_words[:, pair * PAIR * WORDS : (pair + 1) * PAIR * WORDS].rearrange(
-                        "p (j r u) -> p j r u", j=PAIR, u=2
-                    ),
-                    in_=bank[:].rearrange("p (j u r) -> p j r u", j=PAIR, u=2),
-                )
-            return grouped
+        for q, (b0, n, s, i0, T) in enumerate(groups):
+            nc.vector.tensor_copy(
+                out=select[:, q * P : (q + 1) * P].rearrange("k (b j) -> k b j", j=s),
+                in_=ident[:, b0 : b0 + n].unsqueeze(2).to_broadcast([P, n, s]),
+            )
+        for s in spreads:
+            nc.vector.tensor_reduce(
+                out=slot_mask[s][:], in_=ident[:].rearrange("p (b j) -> p j b", j=s), axis=AXIS_X, op=ALU.add
+            )
 
-        def quantise(grouped, codes, scales):
-            nc.vector.quantize_mx(out=codes.bitcast(FP8X4), scales=scales, in_=grouped[:])
+        def transpose_pair(source, first_tile, pool, tag):
+            words = source[:].bitcast(F32)
+            bank = pool.tile([P, PAIR * WORDS], F32, tag=tag)
+            for j in range(PAIR):
+                for u in range(2):
+                    col = (first_tile + j) * WORDS
+                    nc.tensor.transpose(
+                        bank[:, (2 * j + u) * P : (2 * j + u + 1) * P],
+                        words[:, col + u : col + WORDS : 2],
+                        ident[:],
+                    )
+            return bank
 
-        def quantise_text(g, grouped):
-            cols = slice(g * GROUP * P, (g + 1) * GROUP * P)
-            quantise(grouped, x_codes[:, cols], x_scales[:, cols])
+        def copy_pair(copy, bank, grouped, pair):
+            copy(
+                out=grouped[:].bitcast(F32)[:, pair * PAIR * WORDS : (pair + 1) * PAIR * WORDS].rearrange(
+                    "p (j r u) -> p j r u", j=PAIR, u=2
+                ),
+                in_=bank[:].rearrange("p (j u r) -> p j r u", j=PAIR, u=2),
+            )
 
-        def multiply_and_sum(l):
-            acc = psum_acc.tile([P, H], F32)
+        def quantise(grouped, pair, n_pairs, codes, scales, first_col):
+            cols = slice(first_col, first_col + n_pairs * PAIR * P)
+            nc.vector.quantize_mx(
+                out=codes[:, cols].bitcast(FP8X4),
+                scales=scales[:, cols],
+                in_=grouped[:, pair * PAIR * H : (pair + n_pairs) * PAIR * H],
+            )
+
+        def multiply(i):
+            acc = psum_acc.tile([P, H], F32, tag="acc")
             nc.tensor.matmul_mx(
                 out=acc[:],
-                lhsT=x_codes[:, l * P : (l + 1) * P].bitcast(FP8X4),
-                lhsT_scale=x_scales[:, l * P : (l + 1) * P],
+                lhsT=x_codes[:, i * P : (i + 1) * P].bitcast(FP8X4),
+                lhsT_scale=x_scales[:, i * P : (i + 1) * P],
                 rhs=w_codes[:].bitcast(FP8X4),
                 rhs_scale=w_scales[:],
                 start=True,
                 stop=True,
             )
-            nc.vector.scalar_tensor_tensor(
-                out=weighted[:, l, :],
-                in0=acc[:],
-                scalar=2.0,
-                in1=vp[:],
-                op0=ALU.mult,
-                op1=ALU.mult,
-                accum_out=coupling[:, l : l + 1],
-            )
             return acc
 
-        def add_bias_off_vector(l, acc):
-            nc.scalar.copy(out=text_proj[:, l, :], in_=acc[:])
-            nc.gpsimd.tensor_tensor(
-                out=text_proj[:, l, :], in0=text_proj[:, l, :], in1=bias[:], op=ALU.add
+        def vp_of(q):
+            return rows[:, (1 + q) * H : (2 + q) * H]
+
+        def sum_agreement(i, acc):
+            nc.vector.scalar_tensor_tensor(
+                out=weighted[:, i, :],
+                in0=acc[:],
+                scalar=2.0,
+                in1=vp_of(group_of_tile[i]),
+                op0=ALU.mult,
+                op1=ALU.mult,
+                accum_out=coupling[:, i : i + 1],
             )
 
-        def add_bias_on_vector(l, acc):
-            nc.vector.tensor_tensor(out=text_proj[:, l, :], in0=acc[:], in1=bias[:], op=ALU.add)
+        def copy_out(i, acc):
+            nc.scalar.copy(out=text_proj[:, i, :], in_=acc[:])
 
-        def store_text_proj(g):
-            tiles = slice(g * GROUP, (g + 1) * GROUP)
-            nc.sync.dma_start(out=out_0[:, tiles, :], in_=text_proj[:, tiles, :])
+        def bias_gpsimd(i):
+            nc.gpsimd.tensor_tensor(
+                out=text_proj[:, i, :], in0=text_proj[:, i, :], in1=rows[:, 0:H], op=ALU.add
+            )
 
-        quantise(regroup(w_rows, 0, nc.vector.tensor_copy), w_codes[:], w_scales[:])
-        grouped_of = {0: regroup(text_rows, 0, nc.scalar.copy)}
-        quantise_text(0, grouped_of[0])
-        spread = psum_acc.tile([P, H], F32, tag="acc")
-        nc.tensor.matmul(out=spread[:], lhsT=ones[:], rhs=bt_rows[:], start=True, stop=True)
-        nc.scalar.copy(out=bias[:], in_=spread[:])
-        nc.scalar.copy(out=vp[:], in_=vp_bf[:])
-        grouped_of[1] = regroup(text_rows, GROUP, nc.scalar.copy)
-        waiting = []
-        for g in range(N_GROUPS):
-            for j in range(GROUP):
-                l = g * GROUP + j
-                acc = multiply_and_sum(l)
-                if j == 0 and g + 1 < N_GROUPS:
-                    quantise_text(g + 1, grouped_of[g + 1])
-                if j < GPSIMD_SHARE:
-                    add_bias_off_vector(l, acc)
-                elif g < N_GROUPS - 1:
-                    add_bias_on_vector(l, acc)
+        def bias_vector(i, acc):
+            nc.vector.tensor_tensor(out=text_proj[:, i, :], in0=acc[:], in1=rows[:, 0:H], op=ALU.add)
+
+        def store(o, data, first, count):
+            nc.sync.dma_start(out=hbm_tiles(out_flat[o], first, count), in_=data[:, first : first + count, :])
+
+        def spread_rows(bank_no):
+            first = 2 * bank_no
+            last = min(first + 2, 1 + n_groups)
+            bank = psum_misc.tile([P, 2 * H], BF16, tag="misc")
+            for slot in range(first, last):
+                out = bank[:, (slot - first) * H : (slot - first + 1) * H]
+                if slot == 0:
+                    nc.tensor.matmul(out=out, lhsT=ones[:], rhs=bt_rows[:], start=True, stop=True)
                 else:
-                    waiting.append((l, acc))
-            if g < N_GROUPS - 1:
-                store_text_proj(g)
-            if g + 2 < N_GROUPS:
-                grouped_of[g + 2] = regroup(text_rows, (g + 2) * GROUP, nc.scalar.copy)
-
-        nc.vector.tensor_reduce(
-            out=neg_max[:], in_=coupling[:], axis=mybir.AxisListType.X, op=ALU.max, negate=True
-        )
-        nc.scalar.activation(
-            out=exps[:], in_=coupling[:], func=ACT.Exp, bias=neg_max[:], scale=1.0, accum_out=exp_sum[:]
-        )
-        for l, acc in waiting:
-            add_bias_on_vector(l, acc)
-        store_text_proj(N_GROUPS - 1)
-        nc.vector.reciprocal(out=inv_sum[:], in_=exp_sum[:])
-        nc.vector.tensor_scalar(
-            out=routing[:], in0=exps[:], scalar1=inv_sum[:, 0:1], scalar2=None, op0=ALU.mult
-        )
-
-        for g in range(N_GROUPS):
-            for l in range(g * GROUP, (g + 1) * GROUP):
-                if l % 2 == 0:
-                    nc.scalar.activation(
-                        out=weighted[:, l, :], in_=vp[:], func=ACT.Copy, scale=routing[:, l : l + 1]
+                    nc.tensor.matmul(
+                        out=out, lhsT=select[:, (slot - 1) * P : slot * P], rhs=vp_bf[:], start=True, stop=True
                     )
-                else:
-                    nc.vector.tensor_scalar(
-                        out=weighted[:, l, :],
-                        in0=vp[:],
-                        scalar1=routing[:, l : l + 1],
-                        scalar2=None,
-                        op0=ALU.mult,
-                    )
-            tiles = slice(g * GROUP, (g + 1) * GROUP)
-            nc.sync.dma_start(out=out_1[:, tiles, :], in_=weighted[:, tiles, :])
+            nc.scalar.copy(out=rows[:, first * H : last * H], in_=bank[:, : (last - first) * H])
+
+        def softmax_mask(q):
+            b0, n, s, i0, T = groups[q]
+            masked = small.tile([P, L], F32, tag="masked")
+            nc.vector.tensor_tensor(
+                out=masked[:].rearrange("p (j t) -> p j t", j=s),
+                in0=coupling[:, i0 : i0 + T].unsqueeze(1).to_broadcast([P, s, T]),
+                in1=slot_mask[s][:].unsqueeze(2).to_broadcast([P, s, T]),
+                op=ALU.mult,
+            )
+            return masked
+
+        def softmax_gather(q, masked):
+            s = groups[q][2]
+            bank = psum_misc.tile([P, L], F32, tag="misc")
+            nc.tensor.matmul(out=bank[:], lhsT=block[s][:], rhs=masked[:], start=True, stop=True)
+            return bank
+
+        def softmax_max(q, bank):
+            nc.vector.tensor_reduce(out=neg_max[:, q : q + 1], in_=bank[:], axis=AXIS_X, op=ALU.max, negate=True)
+
+        def softmax_exp(q, bank):
+            b0, n, s, i0, T = groups[q]
+            all_exps = small.tile([P, L], F32, tag="all_exps")
+            nc.scalar.activation(
+                out=all_exps[:], in_=bank[:], func=ACT.Exp, bias=neg_max[:, q : q + 1], scale=1.0,
+                accum_out=exp_sum[:, q : q + 1],
+            )
+            nc.scalar.activation(
+                out=exps[:, i0 : i0 + T], in_=coupling[:, i0 : i0 + T], func=ACT.Exp,
+                bias=neg_max[:, q : q + 1], scale=1.0,
+            )
+
+        def softmax_inverse(q):
+            nc.vector.reciprocal(out=inv_sum[:, q : q + 1], in_=exp_sum[:, q : q + 1])
+
+        def softmax_routing(q):
+            b0, n, s, i0, T = groups[q]
+            nc.vector.tensor_scalar(
+                out=routing[:, i0 : i0 + T], in0=exps[:, i0 : i0 + T], scalar1=inv_sum[:, q : q + 1],
+                scalar2=None, op0=ALU.mult,
+            )
+
+        def weigh(engine, i):
+            q = group_of_tile[i]
+            if engine == "scalar":
+                nc.scalar.activation(
+                    out=weighted[:, i, :], in_=vp_of(q), func=ACT.Copy, scale=routing[:, i : i + 1]
+                )
+            elif engine == "gpsimd":
+                nc.gpsimd.tensor_scalar(
+                    out=weighted[:, i, :], in0=vp_of(q), scalar1=exps[:, i : i + 1],
+                    scalar2=inv_sum[:, q : q + 1], op0=ALU.mult, op1=ALU.mult,
+                )
+            else:
+                nc.vector.tensor_scalar(
+                    out=weighted[:, i, :], in0=vp_of(q), scalar1=routing[:, i : i + 1],
+                    scalar2=None, op0=ALU.mult,
+                )
+
+        w_grouped = stage.tile([P, CHUNK * H], BF16, align_bytes=64, tag="grouped")
+        grouped = {0: stage.tile([P, CHUNK * H], BF16, align_bytes=64, tag="grouped", name="grouped0")}
+        w_a = transpose_pair(w_rows, 0, psum_t, "bank")
+        w_b = transpose_pair(w_rows, PAIR, psum_t, "bank")
+        x_a = transpose_pair(text_rows, 0, psum_acc, "acc")
+        copy_pair(nc.vector.tensor_copy, w_a, w_grouped, 0)
+        copy_pair(nc.scalar.copy, w_b, w_grouped, 1)
+        copy_pair(nc.scalar.copy, x_a, grouped[0], 0)
+        quantise(w_grouped, 0, 1, w_codes, w_scales, 0)
+        quantise(w_grouped, 1, 1, w_codes, w_scales, PAIR * P)
+        quantise(grouped[0], 0, 1, x_codes, x_scales, 0)
+        spread_rows(0)
+        x_b = transpose_pair(text_rows, PAIR, psum_acc, "acc")
+        copy_pair(nc.scalar.copy, x_b, grouped[0], 1)
+
+        def regroup(c):
+            grouped[c] = stage.tile([P, CHUNK * H], BF16, align_bytes=64, tag="grouped", name="grouped%d" % c)
+            banks = [transpose_pair(text_rows, c * CHUNK + k * PAIR, psum_t, "bank") for k in range(2)]
+            return banks
+
+        def copy_chunk(c, banks):
+            for k in range(2):
+                copy_pair(nc.scalar.copy, banks[k], grouped[c], k)
+
+        ready = []
+        masked = {}
+        spread_done = 1
+        for c in range(N_CHUNKS):
+            tiles = [c * CHUNK + j for j in range(CHUNK)]
+            q = group_of_tile[tiles[0]]
+            starts_group = groups[q][3] == tiles[0]
+            ends_group = groups[q][3] + groups[q][4] == tiles[-1] + 1
+            soft = q - 1 if starts_group and q > 0 else None
+            last = c == N_CHUNKS - 1
+            next_q = group_of_tile[tiles[-1] + 1] if not last else None
+
+            acc = {}
+            acc[0] = multiply(tiles[0])
+            sum_agreement(tiles[0], acc[0])
+            acc[1] = multiply(tiles[1])
+            if soft is not None:
+                bank = softmax_gather(soft, masked[soft])
+                softmax_max(soft, bank)
+            if c == 0:
+                quantise(grouped[0], 1, 1, x_codes, x_scales, PAIR * P)
+                banks = regroup(1)
+                copy_chunk(1, banks)
+            elif not last:
+                quantise(grouped[c + 1], 0, 2, x_codes, x_scales, (c + 1) * CHUNK * P)
+            plan = ready[:CHUNK] if not last else list(ready)
+            if soft is None:
+                to_gpsimd = plan[3:4]
+                to_scalar = [i for i in plan if i not in to_gpsimd]
+                early = to_scalar[:2]
+            else:
+                early = []
+            for i in early[:1]:
+                weigh("scalar", i)
+            copy_out(tiles[0], acc[0])
+            bias_gpsimd(tiles[0])
+            if soft is not None:
+                softmax_exp(soft, bank)
+            sum_agreement(tiles[1], acc[1])
+            for i in early[1:2]:
+                weigh("scalar", i)
+            copy_out(tiles[1], acc[1])
+            bias_gpsimd(tiles[1])
+            if soft is not None:
+                softmax_inverse(soft)
+                softmax_routing(soft)
+                ready.extend(range(groups[soft][3], groups[soft][3] + groups[soft][4]))
+                plan = ready[:CHUNK] if not last else list(ready)
+                to_gpsimd = plan[3:4]
+            if c == 0:
+                quantise(grouped[1], 0, 2, x_codes, x_scales, CHUNK * P)
+            acc[2] = multiply(tiles[2])
+            acc[3] = multiply(tiles[3])
+            if c + 2 < N_CHUNKS:
+                banks = regroup(c + 2)
+            sum_agreement(tiles[2], acc[2])
+            sum_agreement(tiles[3], acc[3])
+            bias_vector(tiles[2], acc[2])
+            if ends_group:
+                masked[q] = softmax_mask(q)
+            if last:
+                bank = softmax_gather(q, masked[q])
+            bias_vector(tiles[3], acc[3])
+            if c + 2 < N_CHUNKS:
+                copy_chunk(c + 2, banks)
+            if next_q is not None and next_q != q and (1 + next_q) // 2 >= spread_done:
+                spread_rows(spread_done)
+                spread_done += 1
+            for i in to_gpsimd:
+                weigh("gpsimd", i)
+            for i in plan:
+                if i not in to_gpsimd and i not in early:
+                    weigh("scalar", i)
+            ready = [i for i in ready if i not in plan]
+            store(0, text_proj, tiles[0], CHUNK)
+            for k in range(0, len(plan), CHUNK):
+                store(1, weighted, plan[k], CHUNK)
+
+        q = n_groups - 1
+        softmax_max(q, bank)
+        softmax_exp(q, bank)
+        softmax_inverse(q)
+        softmax_routing(q)
+        b0, n, s, i0, T = groups[q]
+        for t in range(0, T, 2):
+            weigh("vector", i0 + t)
+            weigh("scalar" if t % 4 == 0 else "vector", i0 + t + 1)
+            store(1, weighted, i0 + t, 2)

@@ -19,35 +19,14 @@ WORDS = H // 2
 PAIR = 2
 CHUNK = 4
 N_CHUNKS = L // CHUNK
-GROUPS = (16, 32, 32, 32, 16)
-GPSIMD_BIAS = 2
+SPREAD = L // CHUNK
+BATCHES = P // SPREAD
 
 FLOPS = 2 * P * L * H * H
 
 
-def group_table():
-    table = []
-    first_batch = 0
-    first_tile = 0
-    for n in GROUPS:
-        spread = P // n
-        tiles = L // spread
-        table.append((first_batch, n, spread, first_tile, tiles))
-        first_batch += n
-        first_tile += tiles
-    return table
-
-
 def tile_dynamicroutingfusion_pa_t_kernel(tc, text_feat, vision_proj, Wt, bt, out_0, out_1):
     nc = tc.nc
-    groups = group_table()
-    n_groups = len(groups)
-    group_of_tile = {}
-    for q, (b0, n, s, i0, T) in enumerate(groups):
-        for t in range(T):
-            group_of_tile[i0 + t] = q
-    spreads = sorted(set(g[2] for g in groups))
-
     with ExitStack() as ctx:
         keep = ctx.enter_context(tc.tile_pool(name="keep", bufs=1))
         stage = ctx.enter_context(tc.tile_pool(name="stage", bufs=3))
@@ -67,30 +46,27 @@ def tile_dynamicroutingfusion_pa_t_kernel(tc, text_feat, vision_proj, Wt, bt, ou
         x_codes = keep.tile([P, L * P], U32, align_bytes=64)
         x_scales = keep.tile([P, L * P], U8, align_bytes=64)
         vp_bf = keep.tile([P, H], BF16)
-        select = keep.tile([P, n_groups * P], BF16)
-        rows = keep.tile([P, (1 + n_groups) * H], BF16)
+        select = keep.tile([P, N_CHUNKS * P], BF16)
+        rows = keep.tile([P, (1 + N_CHUNKS) * H], BF16)
         text_proj = keep.tile([P, L, H], F32)
         weighted = keep.tile([P, L, H], F32)
         coupling = keep.tile([P, L], F32)
         exps = keep.tile([P, L], F32)
         routing = keep.tile([P, L], F32)
-        neg_max = keep.tile([P, n_groups], F32)
-        exp_sum = keep.tile([P, n_groups], F32)
-        inv_sum = keep.tile([P, n_groups], F32)
+        neg_max = keep.tile([P, N_CHUNKS], F32)
+        exp_sum = keep.tile([P, N_CHUNKS], F32)
+        inv_sum = keep.tile([P, N_CHUNKS], F32)
         warm = keep.tile([P, 1], F32)
-        block = {}
-        slot_mask = {}
-        for s in spreads:
-            block[s] = keep.tile([P, P], F32, name="block%d" % s)
-            slot_mask[s] = keep.tile([P, s], F32, name="slot_mask%d" % s)
+        block = keep.tile([P, P], F32)
+        slot_mask = keep.tile([P, SPREAD], F32)
 
         text_flat = text_feat.rearrange("b l k -> (b l) k")
         out_flat = [o.rearrange("b l h -> (b l) h") for o in (out_0, out_1)]
 
         def hbm_tiles(flat, first, count):
-            b0, n, s, i0, T = groups[group_of_tile[first]]
-            view = flat[b0 * L : (b0 + n) * L, :].rearrange("(p t) k -> p t k", t=T)
-            return view[:, first - i0 : first - i0 + count, :]
+            c, t = divmod(first, CHUNK)
+            view = flat[c * BATCHES * L : (c + 1) * BATCHES * L, :].rearrange("(p t) k -> p t k", t=CHUNK)
+            return view[:, t : t + count, :]
 
         def load_text(first, count):
             nc.sync.dma_start(
@@ -117,29 +93,26 @@ def tile_dynamicroutingfusion_pa_t_kernel(tc, text_feat, vision_proj, Wt, bt, ou
             load_text(c * CHUNK, CHUNK)
 
         make_identity(nc, ident[:])
-        for s in spreads:
-            nc.gpsimd.memset(block[s][:], 0.0)
-            nc.gpsimd.affine_select(
-                out=block[s][:], in_=block[s][:], compare_op=ALU.is_gt, fill=1.0, base=1 - s,
-                pattern=[[-s, P // s], [0, s]], channel_multiplier=1,
-            )
-            nc.gpsimd.affine_select(
-                out=block[s][:], in_=block[s][:], compare_op=ALU.is_ge, fill=0.0, base=0,
-                pattern=[[-s, P // s], [0, s]], channel_multiplier=1,
-            )
+        nc.gpsimd.memset(block[:], 0.0)
+        nc.gpsimd.affine_select(
+            out=block[:], in_=block[:], compare_op=ALU.is_gt, fill=1.0, base=1 - SPREAD,
+            pattern=[[-SPREAD, BATCHES], [0, SPREAD]], channel_multiplier=1,
+        )
+        nc.gpsimd.affine_select(
+            out=block[:], in_=block[:], compare_op=ALU.is_ge, fill=0.0, base=0,
+            pattern=[[-SPREAD, BATCHES], [0, SPREAD]], channel_multiplier=1,
+        )
         nc.vector.memset(ones[:], 1.0)
         nc.vector.memset(warm[:], 0.0)
         nc.scalar.activation(out=warm[:], in_=warm[:], func=ACT.Exp)
 
-        for q, (b0, n, s, i0, T) in enumerate(groups):
-            nc.vector.tensor_copy(
-                out=select[:, q * P : (q + 1) * P].rearrange("k (b j) -> k b j", j=s),
-                in_=ident[:, b0 : b0 + n].unsqueeze(2).to_broadcast([P, n, s]),
-            )
-        for s in spreads:
-            nc.vector.tensor_reduce(
-                out=slot_mask[s][:], in_=ident[:].rearrange("p (b j) -> p j b", j=s), axis=AXIS_X, op=ALU.add
-            )
+        nc.vector.tensor_copy(
+            out=select[:].rearrange("k (b j) -> k b j", j=SPREAD),
+            in_=ident[:].unsqueeze(2).to_broadcast([P, P, SPREAD]),
+        )
+        nc.vector.tensor_reduce(
+            out=slot_mask[:], in_=ident[:].rearrange("p (b j) -> p j b", j=SPREAD), axis=AXIS_X, op=ALU.add
+        )
 
         def transpose_pair(source, first_tile, pool, tag):
             words = source[:].bitcast(F32)
@@ -191,7 +164,7 @@ def tile_dynamicroutingfusion_pa_t_kernel(tc, text_feat, vision_proj, Wt, bt, ou
                 out=weighted[:, i, :],
                 in0=acc[:],
                 scalar=2.0,
-                in1=vp_of(group_of_tile[i]),
+                in1=vp_of(i // CHUNK),
                 op0=ALU.mult,
                 op1=ALU.mult,
                 accum_out=coupling[:, i : i + 1],
@@ -213,7 +186,7 @@ def tile_dynamicroutingfusion_pa_t_kernel(tc, text_feat, vision_proj, Wt, bt, ou
 
         def spread_rows(bank_no):
             first = 2 * bank_no
-            last = min(first + 2, 1 + n_groups)
+            last = min(first + 2, 1 + N_CHUNKS)
             bank = psum_misc.tile([P, 2 * H], BF16, tag="misc")
             for slot in range(first, last):
                 out = bank[:, (slot - first) * H : (slot - first + 1) * H]
@@ -225,174 +198,182 @@ def tile_dynamicroutingfusion_pa_t_kernel(tc, text_feat, vision_proj, Wt, bt, ou
                     )
             nc.scalar.copy(out=rows[:, first * H : last * H], in_=bank[:, : (last - first) * H])
 
-        def softmax_mask(q):
-            b0, n, s, i0, T = groups[q]
+        def softmax_mask(engine, q):
             masked = small.tile([P, L], F32, tag="masked")
-            nc.vector.tensor_tensor(
-                out=masked[:].rearrange("p (j t) -> p j t", j=s),
-                in0=coupling[:, i0 : i0 + T].unsqueeze(1).to_broadcast([P, s, T]),
-                in1=slot_mask[s][:].unsqueeze(2).to_broadcast([P, s, T]),
+            engine.tensor_tensor(
+                out=masked[:].rearrange("p (j t) -> p j t", j=SPREAD),
+                in0=coupling[:, q * CHUNK : (q + 1) * CHUNK].unsqueeze(1).to_broadcast([P, SPREAD, CHUNK]),
+                in1=slot_mask[:].unsqueeze(2).to_broadcast([P, SPREAD, CHUNK]),
                 op=ALU.mult,
             )
             return masked
 
-        def softmax_gather(q, masked):
-            s = groups[q][2]
+        def softmax_gather(masked):
             bank = psum_misc.tile([P, L], F32, tag="misc")
-            nc.tensor.matmul(out=bank[:], lhsT=block[s][:], rhs=masked[:], start=True, stop=True)
+            nc.tensor.matmul(out=bank[:], lhsT=block[:], rhs=masked[:], start=True, stop=True)
             return bank
 
         def softmax_max(q, bank):
             nc.vector.tensor_reduce(out=neg_max[:, q : q + 1], in_=bank[:], axis=AXIS_X, op=ALU.max, negate=True)
 
         def softmax_exp(q, bank):
-            b0, n, s, i0, T = groups[q]
             all_exps = small.tile([P, L], F32, tag="all_exps")
             nc.scalar.activation(
                 out=all_exps[:], in_=bank[:], func=ACT.Exp, bias=neg_max[:, q : q + 1], scale=1.0,
                 accum_out=exp_sum[:, q : q + 1],
             )
+            cols = slice(q * CHUNK, (q + 1) * CHUNK)
             nc.scalar.activation(
-                out=exps[:, i0 : i0 + T], in_=coupling[:, i0 : i0 + T], func=ACT.Exp,
-                bias=neg_max[:, q : q + 1], scale=1.0,
+                out=exps[:, cols], in_=coupling[:, cols], func=ACT.Exp, bias=neg_max[:, q : q + 1], scale=1.0
             )
 
         def softmax_inverse(q):
             nc.vector.reciprocal(out=inv_sum[:, q : q + 1], in_=exp_sum[:, q : q + 1])
 
         def softmax_routing(q):
-            b0, n, s, i0, T = groups[q]
-            nc.vector.tensor_scalar(
-                out=routing[:, i0 : i0 + T], in0=exps[:, i0 : i0 + T], scalar1=inv_sum[:, q : q + 1],
-                scalar2=None, op0=ALU.mult,
+            cols = slice(q * CHUNK, (q + 1) * CHUNK)
+            nc.scalar.activation(
+                out=routing[:, cols], in_=exps[:, cols], func=ACT.Copy, scale=inv_sum[:, q : q + 1]
             )
 
-        def weigh(engine, i):
-            q = group_of_tile[i]
-            if engine == "scalar":
-                nc.scalar.activation(
-                    out=weighted[:, i, :], in_=vp_of(q), func=ACT.Copy, scale=routing[:, i : i + 1]
-                )
-            elif engine == "gpsimd":
-                nc.gpsimd.tensor_scalar(
-                    out=weighted[:, i, :], in0=vp_of(q), scalar1=exps[:, i : i + 1],
-                    scalar2=inv_sum[:, q : q + 1], op0=ALU.mult, op1=ALU.mult,
-                )
-            else:
-                nc.vector.tensor_scalar(
-                    out=weighted[:, i, :], in0=vp_of(q), scalar1=routing[:, i : i + 1],
-                    scalar2=None, op0=ALU.mult,
-                )
+        def weigh_scalar(i):
+            q = i // CHUNK
+            nc.scalar.activation(out=weighted[:, i, :], in_=vp_of(q), func=ACT.Copy, scale=routing[:, i : i + 1])
 
-        w_grouped = stage.tile([P, CHUNK * H], BF16, align_bytes=64, tag="grouped")
-        grouped = {0: stage.tile([P, CHUNK * H], BF16, align_bytes=64, tag="grouped", name="grouped0")}
+        def weigh_two(engine, i):
+            q = i // CHUNK
+            engine.tensor_scalar(
+                out=weighted[:, i, :], in0=vp_of(q), scalar1=exps[:, i : i + 1],
+                scalar2=inv_sum[:, q : q + 1], op0=ALU.mult, op1=ALU.mult,
+            )
+
+        def new_grouped():
+            grouped = stage.tile([P, CHUNK * H], BF16, align_bytes=64, tag="grouped")
+            return grouped
+
+        def transpose_chunk(c):
+            return [transpose_pair(text_rows, c * CHUNK + k * PAIR, psum_t, "bank") for k in range(2)]
+
+        def quantise_chunk(c):
+            quantise(grouped_of[c], 0, 2, x_codes, x_scales, c * CHUNK * P)
+
+        w_grouped = new_grouped()
+        grouped_of = {0: new_grouped()}
         w_a = transpose_pair(w_rows, 0, psum_t, "bank")
         w_b = transpose_pair(w_rows, PAIR, psum_t, "bank")
         x_a = transpose_pair(text_rows, 0, psum_acc, "acc")
         copy_pair(nc.vector.tensor_copy, w_a, w_grouped, 0)
         copy_pair(nc.scalar.copy, w_b, w_grouped, 1)
-        copy_pair(nc.scalar.copy, x_a, grouped[0], 0)
+        copy_pair(nc.scalar.copy, x_a, grouped_of[0], 0)
         quantise(w_grouped, 0, 1, w_codes, w_scales, 0)
         quantise(w_grouped, 1, 1, w_codes, w_scales, PAIR * P)
-        quantise(grouped[0], 0, 1, x_codes, x_scales, 0)
+        quantise(grouped_of[0], 0, 1, x_codes, x_scales, 0)
         spread_rows(0)
         x_b = transpose_pair(text_rows, PAIR, psum_acc, "acc")
-        copy_pair(nc.scalar.copy, x_b, grouped[0], 1)
+        copy_pair(nc.scalar.copy, x_b, grouped_of[0], 1)
+        acc = {0: multiply(0), 1: multiply(1)}
 
-        def regroup(c):
-            grouped[c] = stage.tile([P, CHUNK * H], BF16, align_bytes=64, tag="grouped", name="grouped%d" % c)
-            banks = [transpose_pair(text_rows, c * CHUNK + k * PAIR, psum_t, "bank") for k in range(2)]
-            return banks
+        sum_agreement(0, acc[0])
+        quantise(grouped_of[0], 1, 1, x_codes, x_scales, PAIR * P)
+        grouped_of[1] = new_grouped()
+        banks = transpose_chunk(1)
+        copy_pair(nc.scalar.copy, banks[0], grouped_of[1], 0)
+        copy_pair(nc.scalar.copy, banks[1], grouped_of[1], 1)
+        acc[2] = multiply(2)
+        acc[3] = multiply(3)
+        spread_rows(1)
+        sum_agreement(1, acc[1])
+        bias_vector(0, acc[0])
+        bias_vector(1, acc[1])
+        store(0, text_proj, 0, PAIR)
+        quantise_chunk(1)
+        grouped_of[2] = new_grouped()
+        banks = transpose_chunk(2)
+        copy_pair(nc.scalar.copy, banks[0], grouped_of[2], 0)
+        copy_pair(nc.scalar.copy, banks[1], grouped_of[2], 1)
+        sum_agreement(2, acc[2])
+        sum_agreement(3, acc[3])
+        masked = softmax_mask(nc.gpsimd, 0)
+        copy_out(3, acc[3])
+        bias_gpsimd(3)
+        bias_vector(2, acc[2])
+        store(0, text_proj, PAIR, PAIR)
 
-        def copy_chunk(c, banks):
-            for k in range(2):
-                copy_pair(nc.scalar.copy, banks[k], grouped[c], k)
+        last = N_CHUNKS - 1
+        for c in range(1, last):
+            first = c * CHUNK
+            prev = c - 1
+            acc = [multiply(first + j) for j in range(CHUNK)]
+            bank = softmax_gather(masked)
+            ahead = c + 2 < N_CHUNKS
+            sum_agreement(first, acc[0])
+            quantise_chunk(c + 1)
+            copy_out(first, acc[0])
+            bias_gpsimd(first)
+            softmax_max(prev, bank)
+            softmax_exp(prev, bank)
+            sum_agreement(first + 1, acc[1])
+            softmax_inverse(prev)
+            if ahead:
+                grouped_of[c + 2] = new_grouped()
+                banks = transpose_chunk(c + 2)
+            copy_out(first + 1, acc[1])
+            bias_gpsimd(first + 1)
+            if c % 2 == 1 and (c + 3) // 2 <= N_CHUNKS // 2:
+                spread_rows((c + 3) // 2)
+            softmax_routing(prev)
+            if ahead:
+                copy_pair(nc.scalar.copy, banks[0], grouped_of[c + 2], 0)
+            weigh_scalar(first - CHUNK)
+            sum_agreement(first + 2, acc[2])
+            bias_vector(first + 2, acc[2])
+            sum_agreement(first + 3, acc[3])
+            bias_vector(first + 3, acc[3])
+            masked = softmax_mask(nc.gpsimd, c)
+            if ahead:
+                copy_pair(nc.scalar.copy, banks[1], grouped_of[c + 2], 1)
+            weigh_scalar(first - CHUNK + 1)
+            store(0, text_proj, first, PAIR)
+            store(1, weighted, first - CHUNK, PAIR)
+            weigh_scalar(first - CHUNK + 2)
+            weigh_two(nc.gpsimd, first - CHUNK + 3)
+            store(0, text_proj, first + PAIR, PAIR)
+            store(1, weighted, first - CHUNK + PAIR, PAIR)
 
-        ready = []
-        masked = {}
-        spread_done = 1
-        for c in range(N_CHUNKS):
-            tiles = [c * CHUNK + j for j in range(CHUNK)]
-            q = group_of_tile[tiles[0]]
-            starts_group = groups[q][3] == tiles[0]
-            ends_group = groups[q][3] + groups[q][4] == tiles[-1] + 1
-            soft = q - 1 if starts_group and q > 0 else None
-            last = c == N_CHUNKS - 1
-            next_q = group_of_tile[tiles[-1] + 1] if not last else None
-
-            acc = {}
-            acc[0] = multiply(tiles[0])
-            sum_agreement(tiles[0], acc[0])
-            acc[1] = multiply(tiles[1])
-            if soft is not None:
-                bank = softmax_gather(soft, masked[soft])
-                softmax_max(soft, bank)
-            if c == 0:
-                quantise(grouped[0], 1, 1, x_codes, x_scales, PAIR * P)
-                banks = regroup(1)
-                copy_chunk(1, banks)
-            elif not last:
-                quantise(grouped[c + 1], 0, 2, x_codes, x_scales, (c + 1) * CHUNK * P)
-            plan = ready[:CHUNK] if not last else list(ready)
-            if soft is None:
-                to_gpsimd = plan[3:4]
-                to_scalar = [i for i in plan if i not in to_gpsimd]
-                early = to_scalar[:2]
-            else:
-                early = []
-            for i in early[:1]:
-                weigh("scalar", i)
-            copy_out(tiles[0], acc[0])
-            bias_gpsimd(tiles[0])
-            if soft is not None:
-                softmax_exp(soft, bank)
-            sum_agreement(tiles[1], acc[1])
-            for i in early[1:2]:
-                weigh("scalar", i)
-            copy_out(tiles[1], acc[1])
-            bias_gpsimd(tiles[1])
-            if soft is not None:
-                softmax_inverse(soft)
-                softmax_routing(soft)
-                ready.extend(range(groups[soft][3], groups[soft][3] + groups[soft][4]))
-                plan = ready[:CHUNK] if not last else list(ready)
-                to_gpsimd = plan[3:4]
-            if c == 0:
-                quantise(grouped[1], 0, 2, x_codes, x_scales, CHUNK * P)
-            acc[2] = multiply(tiles[2])
-            acc[3] = multiply(tiles[3])
-            if c + 2 < N_CHUNKS:
-                banks = regroup(c + 2)
-            sum_agreement(tiles[2], acc[2])
-            sum_agreement(tiles[3], acc[3])
-            bias_vector(tiles[2], acc[2])
-            if ends_group:
-                masked[q] = softmax_mask(q)
-            if last:
-                bank = softmax_gather(q, masked[q])
-            bias_vector(tiles[3], acc[3])
-            if c + 2 < N_CHUNKS:
-                copy_chunk(c + 2, banks)
-            if next_q is not None and next_q != q and (1 + next_q) // 2 >= spread_done:
-                spread_rows(spread_done)
-                spread_done += 1
-            for i in to_gpsimd:
-                weigh("gpsimd", i)
-            for i in plan:
-                if i not in to_gpsimd and i not in early:
-                    weigh("scalar", i)
-            ready = [i for i in ready if i not in plan]
-            store(0, text_proj, tiles[0], CHUNK)
-            for k in range(0, len(plan), CHUNK):
-                store(1, weighted, plan[k], CHUNK)
-
-        q = n_groups - 1
-        softmax_max(q, bank)
-        softmax_exp(q, bank)
-        softmax_inverse(q)
-        softmax_routing(q)
-        b0, n, s, i0, T = groups[q]
-        for t in range(0, T, 2):
-            weigh("vector", i0 + t)
-            weigh("scalar" if t % 4 == 0 else "vector", i0 + t + 1)
-            store(1, weighted, i0 + t, 2)
+        first = last * CHUNK
+        prev = last - 1
+        acc = [multiply(first + j) for j in range(CHUNK)]
+        bank = softmax_gather(masked)
+        sum_agreement(first, acc[0])
+        copy_out(first, acc[0])
+        bias_gpsimd(first)
+        softmax_max(prev, bank)
+        softmax_exp(prev, bank)
+        sum_agreement(first + 1, acc[1])
+        softmax_inverse(prev)
+        softmax_routing(prev)
+        weigh_scalar(first - CHUNK)
+        sum_agreement(first + 2, acc[2])
+        weigh_scalar(first - CHUNK + 1)
+        store(1, weighted, first - CHUNK, PAIR)
+        sum_agreement(first + 3, acc[3])
+        masked = softmax_mask(nc.vector, last)
+        bank = softmax_gather(masked)
+        weigh_two(nc.gpsimd, first - CHUNK + 3)
+        bias_vector(first + 1, acc[1])
+        store(0, text_proj, first, PAIR)
+        softmax_max(last, bank)
+        softmax_exp(last, bank)
+        weigh_scalar(first - CHUNK + 2)
+        store(1, weighted, first - CHUNK + PAIR, PAIR)
+        bias_vector(first + 2, acc[2])
+        softmax_inverse(last)
+        softmax_routing(last)
+        bias_vector(first + 3, acc[3])
+        store(0, text_proj, first + PAIR, PAIR)
+        weigh_scalar(first)
+        weigh_two(nc.vector, first + 1)
+        store(1, weighted, first, PAIR)
+        weigh_two(nc.vector, first + 2)
+        weigh_two(nc.vector, first + 3)
+        store(1, weighted, first + PAIR, PAIR)

@@ -19,6 +19,7 @@ WORDS = H // 2
 PAIR = 2
 CHUNK = 4
 N_CHUNKS = L // CHUNK
+WARM_UP = 5
 SPREAD = L // CHUNK
 BATCHES = P // SPREAD
 
@@ -57,6 +58,7 @@ def tile_dynamicroutingfusion_pa_t_kernel(tc, text_feat, vision_proj, Wt, bt, ou
         exp_sum = keep.tile([P, N_CHUNKS], F32)
         inv_sum = keep.tile([P, N_CHUNKS], F32)
         warm = keep.tile([P, 1], F32)
+        zero = keep.tile([P, P], F32)
         block = keep.tile([P, P], F32)
         slot_mask = keep.tile([P, SPREAD], F32)
 
@@ -82,6 +84,10 @@ def tile_dynamicroutingfusion_pa_t_kernel(tc, text_feat, vision_proj, Wt, bt, ou
                 in_=w_source[:, first : first + count, :],
             )
 
+        nc.vector.memset(zero[:], 0.0)
+        warm_bank = psum_misc.tile([P, P], F32, tag="misc")
+        for repeat in range(WARM_UP):
+            nc.tensor.matmul(out=warm_bank[:], lhsT=zero[:], rhs=zero[:], start=True, stop=True)
         nc.vector.memset(bt_rows[:], 0.0)
         load_w(0, PAIR)
         load_w(PAIR, PAIR)

@@ -33,8 +33,8 @@ def tile_dynamicroutingfusion_pa_t_kernel(tc, text_feat, vision_proj, Wt, bt, ou
         stage = ctx.enter_context(tc.tile_pool(name="stage", bufs=3))
         small = ctx.enter_context(tc.tile_pool(name="small", bufs=2))
         psum_t = ctx.enter_context(tc.psum_pool(name="psum_t", bufs=2))
-        psum_acc = ctx.enter_context(tc.psum_pool(name="psum_acc", bufs=5))
-        psum_misc = ctx.enter_context(tc.psum_pool(name="psum_misc", bufs=1))
+        psum_acc = ctx.enter_context(tc.psum_pool(name="psum_acc", bufs=4))
+        psum_misc = ctx.enter_context(tc.psum_pool(name="psum_misc", bufs=2))
         ctx.enter_context(tc.manual_schedule())
 
         ident = keep.tile([P, P], F32)
@@ -91,7 +91,8 @@ def tile_dynamicroutingfusion_pa_t_kernel(tc, text_feat, vision_proj, Wt, bt, ou
         nc.vector.memset(bt_rows[:], 0.0)
         load_w(0, PAIR)
         load_w(PAIR, PAIR)
-        load_text(0, PAIR)
+        load_text(0, 1)
+        load_text(1, 1)
         nc.sync.dma_start(out=bt_rows[0:1, :], in_=bt.rearrange("(o h) -> o h", o=1))
         nc.sync.dma_start(out=vp_bf[:], in_=vision_proj.rearrange("b o h -> b (o h)"))
         load_text(PAIR, PAIR)
@@ -120,10 +121,10 @@ def tile_dynamicroutingfusion_pa_t_kernel(tc, text_feat, vision_proj, Wt, bt, ou
             out=slot_mask[:], in_=ident[:].rearrange("p (b j) -> p j b", j=SPREAD), axis=AXIS_X, op=ALU.add
         )
 
-        def transpose_pair(source, first_tile, pool, tag):
+        def transpose_tiles(source, first_tile, count, pool, tag):
             words = source[:].bitcast(F32)
-            bank = pool.tile([P, PAIR * WORDS], F32, tag=tag)
-            for j in range(PAIR):
+            bank = pool.tile([P, count * WORDS], F32, tag=tag)
+            for j in range(count):
                 for u in range(2):
                     col = (first_tile + j) * WORDS
                     nc.tensor.transpose(
@@ -133,20 +134,20 @@ def tile_dynamicroutingfusion_pa_t_kernel(tc, text_feat, vision_proj, Wt, bt, ou
                     )
             return bank
 
-        def copy_pair(copy, bank, grouped, pair):
+        def copy_tiles(copy, bank, grouped, first_tile, count):
             copy(
-                out=grouped[:].bitcast(F32)[:, pair * PAIR * WORDS : (pair + 1) * PAIR * WORDS].rearrange(
-                    "p (j r u) -> p j r u", j=PAIR, u=2
+                out=grouped[:].bitcast(F32)[:, first_tile * WORDS : (first_tile + count) * WORDS].rearrange(
+                    "p (j r u) -> p j r u", j=count, u=2
                 ),
-                in_=bank[:].rearrange("p (j u r) -> p j r u", j=PAIR, u=2),
+                in_=bank[:].rearrange("p (j u r) -> p j r u", j=count, u=2),
             )
 
-        def quantise(grouped, pair, n_pairs, codes, scales, first_col):
-            cols = slice(first_col, first_col + n_pairs * PAIR * P)
+        def quantise(grouped, first_tile, count, codes, scales, first_col):
+            cols = slice(first_col, first_col + count * P)
             nc.vector.quantize_mx(
                 out=codes[:, cols].bitcast(FP8X4),
                 scales=scales[:, cols],
-                in_=grouped[:, pair * PAIR * H : (pair + n_pairs) * PAIR * H],
+                in_=grouped[:, first_tile * H : (first_tile + count) * H],
             )
 
         def multiply(i):
@@ -190,7 +191,7 @@ def tile_dynamicroutingfusion_pa_t_kernel(tc, text_feat, vision_proj, Wt, bt, ou
         def store(o, data, first, count):
             nc.sync.dma_start(out=hbm_tiles(out_flat[o], first, count), in_=data[:, first : first + count, :])
 
-        def spread_rows(bank_no):
+        def spread_matmul(bank_no):
             first = 2 * bank_no
             last = min(first + 2, 1 + N_CHUNKS)
             bank = psum_misc.tile([P, 2 * H], BF16, tag="misc")
@@ -202,6 +203,11 @@ def tile_dynamicroutingfusion_pa_t_kernel(tc, text_feat, vision_proj, Wt, bt, ou
                     nc.tensor.matmul(
                         out=out, lhsT=select[:, (slot - 1) * P : slot * P], rhs=vp_bf[:], start=True, stop=True
                     )
+            return bank
+
+        def spread_copy(bank_no, bank):
+            first = 2 * bank_no
+            last = min(first + 2, 1 + N_CHUNKS)
             nc.scalar.copy(out=rows[:, first * H : last * H], in_=bank[:, : (last - first) * H])
 
         def softmax_mask(engine, q):
@@ -257,129 +263,139 @@ def tile_dynamicroutingfusion_pa_t_kernel(tc, text_feat, vision_proj, Wt, bt, ou
             grouped = stage.tile([P, CHUNK * H], BF16, align_bytes=64, tag="grouped")
             return grouped
 
-        def transpose_chunk(c):
-            return [transpose_pair(text_rows, c * CHUNK + k * PAIR, psum_t, "bank") for k in range(2)]
-
         def quantise_chunk(c):
-            quantise(grouped_of[c], 0, 2, x_codes, x_scales, c * CHUNK * P)
+            quantise(grouped_of[c], 0, CHUNK, x_codes, x_scales, c * CHUNK * P)
+
+        def transpose_chunk(c):
+            return [transpose_tiles(text_rows, c * CHUNK + k * PAIR, PAIR, psum_t, "bank") for k in range(2)]
+
+        def copy_chunk(c, banks):
+            for k in range(2):
+                copy_tiles(nc.scalar.copy, banks[k], grouped_of[c], k * PAIR, PAIR)
 
         w_grouped = new_grouped()
         grouped_of = {0: new_grouped()}
-        w_a = transpose_pair(w_rows, 0, psum_t, "bank")
-        w_b = transpose_pair(w_rows, PAIR, psum_t, "bank")
-        x_a = transpose_pair(text_rows, 0, psum_acc, "acc")
-        copy_pair(nc.vector.tensor_copy, w_a, w_grouped, 0)
-        copy_pair(nc.scalar.copy, w_b, w_grouped, 1)
-        copy_pair(nc.scalar.copy, x_a, grouped_of[0], 0)
-        quantise(w_grouped, 0, 1, w_codes, w_scales, 0)
-        quantise(w_grouped, 1, 1, w_codes, w_scales, PAIR * P)
-        quantise(grouped_of[0], 0, 1, x_codes, x_scales, 0)
-        spread_rows(0)
-        x_b = transpose_pair(text_rows, PAIR, psum_acc, "acc")
-        copy_pair(nc.scalar.copy, x_b, grouped_of[0], 1)
-        acc = {0: multiply(0), 1: multiply(1)}
+        w_banks = [transpose_tiles(w_rows, t, 1, psum_t, "bank") for t in range(2)]
+        w_banks.extend([transpose_tiles(w_rows, t, 1, psum_acc, "acc") for t in range(2, CHUNK)])
+        x_banks = [transpose_tiles(text_rows, t, 1, psum_acc, "acc") for t in range(2)]
+        spread = {0: spread_matmul(0)}
+        for t in range(CHUNK):
+            copy_tiles(nc.vector.tensor_copy if t % 2 == 0 else nc.scalar.copy, w_banks[t], w_grouped, t, 1)
+        for t in range(2):
+            copy_tiles(nc.scalar.copy, x_banks[t], grouped_of[0], t, 1)
+        for k in range(2):
+            quantise(w_grouped, k * PAIR, PAIR, w_codes, w_scales, k * PAIR * P)
+        for t in range(2):
+            quantise(grouped_of[0], t, 1, x_codes, x_scales, t * P)
+        spread_copy(0, spread[0])
+        x_bank = transpose_tiles(text_rows, PAIR, PAIR, psum_acc, "acc")
+        copy_tiles(nc.scalar.copy, x_bank, grouped_of[0], PAIR, PAIR)
+        acc = [multiply(0), multiply(1)]
 
+        spread[1] = spread_matmul(1)
+        spread_copy(1, spread[1])
         sum_agreement(0, acc[0])
-        quantise(grouped_of[0], 1, 1, x_codes, x_scales, PAIR * P)
+        copy_out(0, acc[0])
+        bias_gpsimd(0)
+        quantise(grouped_of[0], PAIR, PAIR, x_codes, x_scales, PAIR * P)
         grouped_of[1] = new_grouped()
         banks = transpose_chunk(1)
-        copy_pair(nc.scalar.copy, banks[0], grouped_of[1], 0)
-        copy_pair(nc.scalar.copy, banks[1], grouped_of[1], 1)
-        acc[2] = multiply(2)
-        acc[3] = multiply(3)
-        spread_rows(1)
+        acc.extend([multiply(2), multiply(3)])
+        copy_chunk(1, banks)
+        spread[2] = spread_matmul(2)
+        spread_copy(2, spread[2])
         sum_agreement(1, acc[1])
-        bias_vector(0, acc[0])
         bias_vector(1, acc[1])
         store(0, text_proj, 0, PAIR)
+        sum_agreement(2, acc[2])
+        bias_vector(2, acc[2])
         quantise_chunk(1)
         grouped_of[2] = new_grouped()
         banks = transpose_chunk(2)
-        copy_pair(nc.scalar.copy, banks[0], grouped_of[2], 0)
-        copy_pair(nc.scalar.copy, banks[1], grouped_of[2], 1)
-        sum_agreement(2, acc[2])
+        copy_chunk(2, banks)
+        spread[3] = spread_matmul(3)
+        spread_copy(3, spread[3])
         sum_agreement(3, acc[3])
-        masked = softmax_mask(nc.gpsimd, 0)
-        copy_out(3, acc[3])
-        bias_gpsimd(3)
-        bias_vector(2, acc[2])
+        bias_vector(3, acc[3])
         store(0, text_proj, PAIR, PAIR)
+        masked = softmax_mask(nc.gpsimd, 0)
 
         last = N_CHUNKS - 1
         for c in range(1, last):
             first = c * CHUNK
-            prev = c - 1
-            acc = [multiply(first + j) for j in range(CHUNK)]
+            done = first - CHUNK
+            acc = [multiply(first), multiply(first + 1)]
             bank = softmax_gather(masked)
-            ahead = c + 2 < N_CHUNKS
-            sum_agreement(first, acc[0])
-            quantise_chunk(c + 1)
-            copy_out(first, acc[0])
-            bias_gpsimd(first)
-            softmax_max(prev, bank)
-            softmax_exp(prev, bank)
-            sum_agreement(first + 1, acc[1])
-            softmax_inverse(prev)
-            if ahead:
+            if c == 1:
+                spread[4] = spread_matmul(4)
+            acc.append(multiply(first + 2))
+            if c + 2 < N_CHUNKS:
                 grouped_of[c + 2] = new_grouped()
                 banks = transpose_chunk(c + 2)
-            copy_out(first + 1, acc[1])
-            bias_gpsimd(first + 1)
-            if c % 2 == 1 and (c + 3) // 2 <= N_CHUNKS // 2:
-                spread_rows((c + 3) // 2)
-            softmax_routing(prev)
-            if ahead:
-                copy_pair(nc.scalar.copy, banks[0], grouped_of[c + 2], 0)
-            weigh_scalar(first - CHUNK)
+            acc.append(multiply(first + 3))
+            for j in range(2):
+                sum_agreement(first + j, acc[j])
+                copy_out(first + j, acc[j])
+                bias_gpsimd(first + j)
+            quantise_chunk(c + 1)
+            softmax_max(c - 1, bank)
+            softmax_exp(c - 1, bank)
             sum_agreement(first + 2, acc[2])
             bias_vector(first + 2, acc[2])
+            if c + 2 < N_CHUNKS:
+                copy_chunk(c + 2, banks)
+            softmax_inverse(c - 1)
+            softmax_routing(c - 1)
+            if c == 1:
+                spread_copy(4, spread[4])
+            on_gpsimd = 1 if c == 1 else 2
+            for j in range(CHUNK - on_gpsimd):
+                weigh_scalar(done + j)
             sum_agreement(first + 3, acc[3])
             bias_vector(first + 3, acc[3])
             masked = softmax_mask(nc.gpsimd, c)
-            if ahead:
-                copy_pair(nc.scalar.copy, banks[1], grouped_of[c + 2], 1)
-            weigh_scalar(first - CHUNK + 1)
-            store(0, text_proj, first, PAIR)
-            store(1, weighted, first - CHUNK, PAIR)
-            weigh_scalar(first - CHUNK + 2)
-            weigh_two(nc.gpsimd, first - CHUNK + 3)
-            store(0, text_proj, first + PAIR, PAIR)
-            store(1, weighted, first - CHUNK + PAIR, PAIR)
+            for j in range(CHUNK - on_gpsimd, CHUNK):
+                weigh_two(nc.gpsimd, done + j)
+            pieces = 2 if c == 1 else 1
+            for k in range(pieces):
+                count = CHUNK // pieces
+                store(0, text_proj, first + k * count, count)
+                store(1, weighted, done + k * count, count)
 
         first = last * CHUNK
-        prev = last - 1
-        acc = [multiply(first + j) for j in range(CHUNK)]
+        done = first - CHUNK
+        acc = [multiply(first + j) for j in range(3)]
         bank = softmax_gather(masked)
+        acc.append(multiply(first + 3))
         sum_agreement(first, acc[0])
         copy_out(first, acc[0])
         bias_gpsimd(first)
-        softmax_max(prev, bank)
-        softmax_exp(prev, bank)
         sum_agreement(first + 1, acc[1])
-        softmax_inverse(prev)
-        softmax_routing(prev)
-        weigh_scalar(first - CHUNK)
-        sum_agreement(first + 2, acc[2])
-        weigh_scalar(first - CHUNK + 1)
-        store(1, weighted, first - CHUNK, PAIR)
-        sum_agreement(first + 3, acc[3])
-        masked = softmax_mask(nc.vector, last)
-        bank = softmax_gather(masked)
-        weigh_two(nc.gpsimd, first - CHUNK + 3)
         bias_vector(first + 1, acc[1])
         store(0, text_proj, first, PAIR)
-        softmax_max(last, bank)
-        softmax_exp(last, bank)
-        weigh_scalar(first - CHUNK + 2)
-        store(1, weighted, first - CHUNK + PAIR, PAIR)
+        softmax_max(last - 1, bank)
+        softmax_exp(last - 1, bank)
+        sum_agreement(first + 2, acc[2])
         bias_vector(first + 2, acc[2])
-        softmax_inverse(last)
-        softmax_routing(last)
+        sum_agreement(first + 3, acc[3])
+        softmax_inverse(last - 1)
+        softmax_routing(last - 1)
+        for j in range(2):
+            weigh_scalar(done + j)
+        store(1, weighted, done, PAIR)
+        for j in range(2, CHUNK):
+            weigh_two(nc.gpsimd, done + j)
+        masked = softmax_mask(nc.vector, last)
+        bank = softmax_gather(masked)
         bias_vector(first + 3, acc[3])
         store(0, text_proj, first + PAIR, PAIR)
+        store(1, weighted, done + PAIR, PAIR)
+        softmax_max(last, bank)
+        softmax_exp(last, bank)
+        softmax_inverse(last)
+        softmax_routing(last)
         weigh_scalar(first)
-        weigh_two(nc.vector, first + 1)
-        store(1, weighted, first, PAIR)
-        weigh_two(nc.vector, first + 2)
-        weigh_two(nc.vector, first + 3)
-        store(1, weighted, first + PAIR, PAIR)
+        for j in range(1, CHUNK):
+            weigh_two(nc.vector, first + j)
+        for k in range(2):
+            store(1, weighted, first + k * PAIR, PAIR)

@@ -348,14 +348,12 @@ def tile_dynamicroutingfusion_pa_t_kernel(tc, text_feat, vision_proj, Wt, bt, ou
             softmax_routing(c - 1)
             if c == 1:
                 spread_copy(4, spread[4])
-            on_gpsimd = 1 if c == 1 else 2
-            for j in range(CHUNK - on_gpsimd):
+            for j in range(CHUNK - 1):
                 weigh_scalar(done + j)
             sum_agreement(first + 3, acc[3])
             bias_vector(first + 3, acc[3])
             masked = softmax_mask(nc.gpsimd, c)
-            for j in range(CHUNK - on_gpsimd, CHUNK):
-                weigh_two(nc.gpsimd, done + j)
+            weigh_two(nc.gpsimd, done + CHUNK - 1)
             pieces = 2 if c == 1 else 1
             for k in range(pieces):
                 count = CHUNK // pieces

@@ -325,10 +325,10 @@ def tile_dynamicroutingfusion_pa_t_kernel(tc, text_feat, vision_proj, Wt, bt, ou
             first = c * CHUNK
             done = first - CHUNK
             acc = [multiply(first), multiply(first + 1)]
+            acc.append(multiply(first + 2))
             bank = softmax_gather(masked)
             if c == 1:
                 spread[4] = spread_matmul(4)
-            acc.append(multiply(first + 2))
             if c + 2 < N_CHUNKS:
                 grouped_of[c + 2] = new_grouped()
                 banks = transpose_chunk(c + 2)
@@ -395,5 +395,4 @@ def tile_dynamicroutingfusion_pa_t_kernel(tc, text_feat, vision_proj, Wt, bt, ou
         weigh_scalar(first)
         for j in range(1, CHUNK):
             weigh_two(nc.vector, first + j)
-        for k in range(2):
-            store(1, weighted, first + k * PAIR, PAIR)
+        store(1, weighted, first, CHUNK)

@@ -152,15 +152,16 @@ def tile_dynamicroutingfusion_pa_t_kernel(tc, text_feat, vision_proj, Wt, bt, ou
 
         def multiply(i):
             acc = psum_acc.tile([P, H], F32, tag="acc")
-            nc.tensor.matmul_mx(
-                out=acc[:],
-                lhsT=x_codes[:, i * P : (i + 1) * P].bitcast(FP8X4),
-                lhsT_scale=x_scales[:, i * P : (i + 1) * P],
-                rhs=w_codes[:].bitcast(FP8X4),
-                rhs_scale=w_scales[:],
-                start=True,
-                stop=True,
-            )
+            for repeat in range(3 if i % 4 == 2 and i >= 8 else 1):
+                nc.tensor.matmul_mx(
+                    out=acc[:],
+                    lhsT=x_codes[:, i * P : (i + 1) * P].bitcast(FP8X4),
+                    lhsT_scale=x_scales[:, i * P : (i + 1) * P],
+                    rhs=w_codes[:].bitcast(FP8X4),
+                    rhs_scale=w_scales[:],
+                    start=True,
+                    stop=True,
+                )
             return acc
 
         def vp_of(q):

from contextlib import ExitStack

import concourse.mybir as mybir
from concourse.masks import make_identity

F32 = mybir.dt.float32
BF16 = mybir.dt.bfloat16
U32 = mybir.dt.uint32
U8 = mybir.dt.uint8
FP8X4 = mybir.dt.float8_e4m3fn_x4
ALU = mybir.AluOpType
ACT = mybir.ActivationFunctionType
AXIS_X = mybir.AxisListType.X

P = 128
L = 32
H = 512
WORDS = H // 2
PAIR = 2
CHUNK = 4
N_CHUNKS = L // CHUNK
WARM_UP = 5
SPREAD = L // CHUNK
BATCHES = P // SPREAD

FLOPS = 2 * P * L * H * H


def tile_dynamicroutingfusion_pa_t_kernel(tc, text_feat, vision_proj, Wt, bt, out_0, out_1):
    nc = tc.nc
    with ExitStack() as ctx:
        keep = ctx.enter_context(tc.tile_pool(name="keep", bufs=1))
        stage = ctx.enter_context(tc.tile_pool(name="stage", bufs=3))
        small = ctx.enter_context(tc.tile_pool(name="small", bufs=2))
        psum_t = ctx.enter_context(tc.psum_pool(name="psum_t", bufs=2))
        psum_acc = ctx.enter_context(tc.psum_pool(name="psum_acc", bufs=4))
        psum_misc = ctx.enter_context(tc.psum_pool(name="psum_misc", bufs=2))
        ctx.enter_context(tc.manual_schedule())

        ident = keep.tile([P, P], F32)
        ones = keep.tile([P, P], BF16)
        bt_rows = keep.tile([P, H], BF16)
        w_rows = keep.tile([P, CHUNK * H], BF16)
        w_codes = keep.tile([P, H], U32, align_bytes=64)
        w_scales = keep.tile([P, H], U8, align_bytes=64)
        text_rows = keep.tile([P, L * H], BF16)
        x_codes = keep.tile([P, L * P], U32, align_bytes=64)
        x_scales = keep.tile([P, L * P], U8, align_bytes=64)
        vp_bf = keep.tile([P, H], BF16)
        select = keep.tile([P, N_CHUNKS * P], BF16)
        rows = keep.tile([P, (1 + N_CHUNKS) * H], BF16)
        text_proj = keep.tile([P, L, H], F32)
        weighted = keep.tile([P, L, H], F32)
        coupling = keep.tile([P, L], F32)
        exps = keep.tile([P, L], F32)
        routing = keep.tile([P, L], F32)
        neg_max = keep.tile([P, N_CHUNKS], F32)
        exp_sum = keep.tile([P, N_CHUNKS], F32)
        inv_sum = keep.tile([P, N_CHUNKS], F32)
        warm = keep.tile([P, 1], F32)
        zero = keep.tile([P, P], F32)
        block = keep.tile([P, P], F32)
        slot_mask = keep.tile([P, SPREAD], F32)

        text_flat = text_feat.rearrange("b l k -> (b l) k")
        out_flat = [o.rearrange("b l h -> (b l) h") for o in (out_0, out_1)]

        def hbm_tiles(flat, first, count):
            c, t = divmod(first, CHUNK)
            view = flat[c * BATCHES * L : (c + 1) * BATCHES * L, :].rearrange("(p t) k -> p t k", t=CHUNK)
            return view[:, t : t + count, :]

        def load_text(first, count):
            nc.sync.dma_start(
                out=text_rows[:, first * H : (first + count) * H].rearrange("p (c k) -> p c k", c=count),
                in_=hbm_tiles(text_flat, first, count),
            )

        w_source = Wt.rearrange("(c p) k -> p c k", p=P)

        def load_w(first, count):
            nc.sync.dma_start(
                out=w_rows[:, first * H : (first + count) * H].rearrange("p (c k) -> p c k", c=count),
                in_=w_source[:, first : first + count, :],
            )

        nc.vector.memset(zero[:], 0.0)
        warm_bank = psum_misc.tile([P, P], F32, tag="misc")
        for repeat in range(WARM_UP):
            nc.tensor.matmul(out=warm_bank[:], lhsT=zero[:], rhs=zero[:], start=True, stop=True)
        nc.vector.memset(bt_rows[:], 0.0)
        load_w(0, PAIR)
        load_w(PAIR, PAIR)
        load_text(0, 1)
        load_text(1, 1)
        nc.sync.dma_start(out=bt_rows[0:1, :], in_=bt.rearrange("(o h) -> o h", o=1))
        nc.sync.dma_start(out=vp_bf[:], in_=vision_proj.rearrange("b o h -> b (o h)"))
        load_text(PAIR, PAIR)
        for c in range(1, N_CHUNKS):
            load_text(c * CHUNK, CHUNK)

        make_identity(nc, ident[:])
        nc.gpsimd.memset(block[:], 0.0)
        nc.gpsimd.affine_select(
            out=block[:], in_=block[:], compare_op=ALU.is_gt, fill=1.0, base=1 - SPREAD,
            pattern=[[-SPREAD, BATCHES], [0, SPREAD]], channel_multiplier=1,
        )
        nc.gpsimd.affine_select(
            out=block[:], in_=block[:], compare_op=ALU.is_ge, fill=0.0, base=0,
            pattern=[[-SPREAD, BATCHES], [0, SPREAD]], channel_multiplier=1,
        )
        nc.vector.memset(ones[:], 1.0)
        nc.vector.memset(warm[:], 0.0)
        nc.scalar.activation(out=warm[:], in_=warm[:], func=ACT.Exp)

        nc.vector.tensor_copy(
            out=select[:].rearrange("k (b j) -> k b j", j=SPREAD),
            in_=ident[:].unsqueeze(2).to_broadcast([P, P, SPREAD]),
        )
        nc.vector.tensor_reduce(
            out=slot_mask[:], in_=ident[:].rearrange("p (b j) -> p j b", j=SPREAD), axis=AXIS_X, op=ALU.add
        )

        def transpose_tiles(source, first_tile, count, pool, tag):
            words = source[:].bitcast(F32)
            bank = pool.tile([P, count * WORDS], F32, tag=tag)
            for j in range(count):
                for u in range(2):
                    col = (first_tile + j) * WORDS
                    nc.tensor.transpose(
                        bank[:, (2 * j + u) * P : (2 * j + u + 1) * P],
                        words[:, col + u : col + WORDS : 2],
                        ident[:],
                    )
            return bank

        def copy_tiles(copy, bank, grouped, first_tile, count):
            copy(
                out=grouped[:].bitcast(F32)[:, first_tile * WORDS : (first_tile + count) * WORDS].rearrange(
                    "p (j r u) -> p j r u", j=count, u=2
                ),
                in_=bank[:].rearrange("p (j u r) -> p j r u", j=count, u=2),
            )

        def quantise(grouped, first_tile, count, codes, scales, first_col):
            cols = slice(first_col, first_col + count * P)
            nc.vector.quantize_mx(
                out=codes[:, cols].bitcast(FP8X4),
                scales=scales[:, cols],
                in_=grouped[:, first_tile * H : (first_tile + count) * H],
            )

        def multiply(i):
            acc = psum_acc.tile([P, H], F32, tag="acc")
            for repeat in range(3 if i % 4 == 2 and i >= 8 else 1):
                nc.tensor.matmul_mx(
                    out=acc[:],
                    lhsT=x_codes[:, i * P : (i + 1) * P].bitcast(FP8X4),
                    lhsT_scale=x_scales[:, i * P : (i + 1) * P],
                    rhs=w_codes[:].bitcast(FP8X4),
                    rhs_scale=w_scales[:],
                    start=True,
                    stop=True,
                )
            return acc

        def vp_of(q):
            return rows[:, (1 + q) * H : (2 + q) * H]

        def sum_agreement(i, acc):
            nc.vector.scalar_tensor_tensor(
                out=weighted[:, i, :],
                in0=acc[:],
                scalar=2.0,
                in1=vp_of(i // CHUNK),
                op0=ALU.mult,
                op1=ALU.mult,
                accum_out=coupling[:, i : i + 1],
            )

        def copy_out(i, acc):
            nc.scalar.copy(out=text_proj[:, i, :], in_=acc[:])

        def bias_gpsimd(i):
            nc.gpsimd.tensor_tensor(
                out=text_proj[:, i, :], in0=text_proj[:, i, :], in1=rows[:, 0:H], op=ALU.add
            )

        def bias_vector(i, acc):
            nc.vector.tensor_tensor(out=text_proj[:, i, :], in0=acc[:], in1=rows[:, 0:H], op=ALU.add)

        def store(o, data, first, count):
            nc.sync.dma_start(out=hbm_tiles(out_flat[o], first, count), in_=data[:, first : first + count, :])

        def spread_matmul(bank_no):
            first = 2 * bank_no
            last = min(first + 2, 1 + N_CHUNKS)
            bank = psum_misc.tile([P, 2 * H], BF16, tag="misc")
            for slot in range(first, last):
                out = bank[:, (slot - first) * H : (slot - first + 1) * H]
                if slot == 0:
                    nc.tensor.matmul(out=out, lhsT=ones[:], rhs=bt_rows[:], start=True, stop=True)
                else:
                    nc.tensor.matmul(
                        out=out, lhsT=select[:, (slot - 1) * P : slot * P], rhs=vp_bf[:], start=True, stop=True
                    )
            return bank

        def spread_copy(bank_no, bank):
            first = 2 * bank_no
            last = min(first + 2, 1 + N_CHUNKS)
            nc.scalar.copy(out=rows[:, first * H : last * H], in_=bank[:, : (last - first) * H])

        def softmax_mask(engine, q):
            masked = small.tile([P, L], F32, tag="masked")
            engine.tensor_tensor(
                out=masked[:].rearrange("p (j t) -> p j t", j=SPREAD),
                in0=coupling[:, q * CHUNK : (q + 1) * CHUNK].unsqueeze(1).to_broadcast([P, SPREAD, CHUNK]),
                in1=slot_mask[:].unsqueeze(2).to_broadcast([P, SPREAD, CHUNK]),
                op=ALU.mult,
            )
            return masked

        def softmax_gather(masked):
            bank = psum_misc.tile([P, L], F32, tag="misc")
            nc.tensor.matmul(out=bank[:], lhsT=block[:], rhs=masked[:], start=True, stop=True)
            return bank

        def softmax_max(q, bank):
            nc.vector.tensor_reduce(out=neg_max[:, q : q + 1], in_=bank[:], axis=AXIS_X, op=ALU.max, negate=True)

        def softmax_exp(q, bank):
            all_exps = small.tile([P, L], F32, tag="all_exps")
            nc.scalar.activation(
                out=all_exps[:], in_=bank[:], func=ACT.Exp, bias=neg_max[:, q : q + 1], scale=1.0,
                accum_out=exp_sum[:, q : q + 1],
            )
            cols = slice(q * CHUNK, (q + 1) * CHUNK)
            nc.scalar.activation(
                out=exps[:, cols], in_=coupling[:, cols], func=ACT.Exp, bias=neg_max[:, q : q + 1], scale=1.0
            )

        def softmax_inverse(q):
            nc.vector.reciprocal(out=inv_sum[:, q : q + 1], in_=exp_sum[:, q : q + 1])

        def softmax_routing(q):
            cols = slice(q * CHUNK, (q + 1) * CHUNK)
            nc.scalar.activation(
                out=routing[:, cols], in_=exps[:, cols], func=ACT.Copy, scale=inv_sum[:, q : q + 1]
            )

        def weigh_scalar(i):
            q = i // CHUNK
            nc.scalar.activation(out=weighted[:, i, :], in_=vp_of(q), func=ACT.Copy, scale=routing[:, i : i + 1])

        def weigh_two(engine, i):
            q = i // CHUNK
            engine.tensor_scalar(
                out=weighted[:, i, :], in0=vp_of(q), scalar1=exps[:, i : i + 1],
                scalar2=inv_sum[:, q : q + 1], op0=ALU.mult, op1=ALU.mult,
            )

        def new_grouped():
            grouped = stage.tile([P, CHUNK * H], BF16, align_bytes=64, tag="grouped")
            return grouped

        def quantise_chunk(c):
            quantise(grouped_of[c], 0, CHUNK, x_codes, x_scales, c * CHUNK * P)

        def transpose_chunk(c):
            return [transpose_tiles(text_rows, c * CHUNK + k * PAIR, PAIR, psum_t, "bank") for k in range(2)]

        def copy_chunk(c, banks):
            for k in range(2):
                copy_tiles(nc.scalar.copy, banks[k], grouped_of[c], k * PAIR, PAIR)

        w_grouped = new_grouped()
        grouped_of = {0: new_grouped()}
        w_banks = [transpose_tiles(w_rows, t, 1, psum_t, "bank") for t in range(2)]
        w_banks.extend([transpose_tiles(w_rows, t, 1, psum_acc, "acc") for t in range(2, CHUNK)])
        x_banks = [transpose_tiles(text_rows, t, 1, psum_acc, "acc") for t in range(2)]
        spread = {0: spread_matmul(0)}
        for t in range(CHUNK):
            copy_tiles(nc.vector.tensor_copy if t % 2 == 0 else nc.scalar.copy, w_banks[t], w_grouped, t, 1)
        for t in range(2):
            copy_tiles(nc.scalar.copy, x_banks[t], grouped_of[0], t, 1)
        for k in range(2):
            quantise(w_grouped, k * PAIR, PAIR, w_codes, w_scales, k * PAIR * P)
        for t in range(2):
            quantise(grouped_of[0], t, 1, x_codes, x_scales, t * P)
        spread_copy(0, spread[0])
        x_bank = transpose_tiles(text_rows, PAIR, PAIR, psum_acc, "acc")
        copy_tiles(nc.scalar.copy, x_bank, grouped_of[0], PAIR, PAIR)
        acc = [multiply(0), multiply(1)]

        spread[1] = spread_matmul(1)
        spread_copy(1, spread[1])
        sum_agreement(0, acc[0])
        copy_out(0, acc[0])
        bias_gpsimd(0)
        quantise(grouped_of[0], PAIR, PAIR, x_codes, x_scales, PAIR * P)
        grouped_of[1] = new_grouped()
        banks = transpose_chunk(1)
        acc.extend([multiply(2), multiply(3)])
        copy_chunk(1, banks)
        spread[2] = spread_matmul(2)
        spread_copy(2, spread[2])
        sum_agreement(1, acc[1])
        bias_vector(1, acc[1])
        store(0, text_proj, 0, PAIR)
        sum_agreement(2, acc[2])
        bias_vector(2, acc[2])
        quantise_chunk(1)
        grouped_of[2] = new_grouped()
        banks = transpose_chunk(2)
        copy_chunk(2, banks)
        spread[3] = spread_matmul(3)
        spread_copy(3, spread[3])
        sum_agreement(3, acc[3])
        bias_vector(3, acc[3])
        store(0, text_proj, PAIR, PAIR)
        masked = softmax_mask(nc.gpsimd, 0)

        last = N_CHUNKS - 1
        for c in range(1, last):
            first = c * CHUNK
            done = first - CHUNK
            acc = [multiply(first), multiply(first + 1)]
            acc.append(multiply(first + 2))
            bank = softmax_gather(masked)
            if c == 1:
                spread[4] = spread_matmul(4)
            if c + 2 < N_CHUNKS:
                grouped_of[c + 2] = new_grouped()
                banks = transpose_chunk(c + 2)
            acc.append(multiply(first + 3))
            for j in range(2):
                sum_agreement(first + j, acc[j])
                copy_out(first + j, acc[j])
                bias_gpsimd(first + j)
            quantise_chunk(c + 1)
            softmax_max(c - 1, bank)
            softmax_exp(c - 1, bank)
            sum_agreement(first + 2, acc[2])
            bias_vector(first + 2, acc[2])
            if c + 2 < N_CHUNKS:
                copy_chunk(c + 2, banks)
            softmax_inverse(c - 1)
            softmax_routing(c - 1)
            if c == 1:
                spread_copy(4, spread[4])
            for j in range(CHUNK - 1):
                weigh_scalar(done + j)
            sum_agreement(first + 3, acc[3])
            bias_vector(first + 3, acc[3])
            masked = softmax_mask(nc.gpsimd, c)
            weigh_two(nc.gpsimd, done + CHUNK - 1)
            pieces = 2 if c == 1 else 1
            for k in range(pieces):
                count = CHUNK // pieces
                store(0, text_proj, first + k * count, count)
                store(1, weighted, done + k * count, count)

        first = last * CHUNK
        done = first - CHUNK
        acc = [multiply(first + j) for j in range(3)]
        bank = softmax_gather(masked)
        acc.append(multiply(first + 3))
        sum_agreement(first, acc[0])
        copy_out(first, acc[0])
        bias_gpsimd(first)
        sum_agreement(first + 1, acc[1])
        bias_vector(first + 1, acc[1])
        store(0, text_proj, first, PAIR)
        softmax_max(last - 1, bank)
        softmax_exp(last - 1, bank)
        sum_agreement(first + 2, acc[2])
        bias_vector(first + 2, acc[2])
        sum_agreement(first + 3, acc[3])
        softmax_inverse(last - 1)
        softmax_routing(last - 1)
        for j in range(2):
            weigh_scalar(done + j)
        store(1, weighted, done, PAIR)
        for j in range(2, CHUNK):
            weigh_two(nc.gpsimd, done + j)
        masked = softmax_mask(nc.vector, last)
        bank = softmax_gather(masked)
        bias_vector(first + 3, acc[3])
        store(0, text_proj, first + PAIR, PAIR)
        store(1, weighted, done + PAIR, PAIR)
        softmax_max(last, bank)
        softmax_exp(last, bank)
        softmax_inverse(last)
        softmax_routing(last)
        weigh_scalar(first)
        for j in range(1, CHUNK):
            weigh_two(nc.vector, first + j)
        store(1, weighted, first, CHUNK)
